import numpy as np
import ml_dtypes


def mxq(x, axis, fmt="e4m3"):
    dtype, down = {"e4m3": (ml_dtypes.float8_e4m3fn, 7), "e5m2": (ml_dtypes.float8_e5m2, 14)}[fmt]
    v = np.moveaxis(np.asarray(x, np.float32).astype(ml_dtypes.bfloat16).astype(np.float64), axis, -1)
    blocks = v.reshape(v.shape[:-1] + (-1, 32))
    amax = np.abs(blocks).max(-1, keepdims=True)
    byte = np.maximum(np.where(amax > 0, np.frexp(amax)[1] - 1 + 127, 0) - down, 1)
    scale = np.exp2(byte - 127.0)
    codes = (blocks / scale).astype(np.float32).astype(dtype).astype(np.float64)
    return np.moveaxis((codes * scale).reshape(v.shape), -1, axis)


WIDE = False


def mx_kscale(k):
    if not WIDE:
        return np.ones(k)
    levels = np.array([10, -10, 5, -5, 0])
    a = np.random.permutation(np.resize(levels, k // 512 * 4)).reshape(k // 512, 4)
    idx = np.arange(k)
    return np.exp2(a[idx // 512, idx % 128 // 32])


BF16 = ml_dtypes.bfloat16


def bf(x):
    return np.asarray(x, np.float32).astype(BF16)


def f64(x):
    return np.asarray(x).astype(np.float64)


B, SQ, SK, D, DV = 1, 4096, 512, 128, 1024


def setup_inputs():
    t = mx_kscale(SK)
    return {"qk": bf(1.0 + 0.1 * np.random.standard_normal((1, 1))),
            "qk_scaling_factor": bf(1.5 + 0.1 * np.random.standard_normal((1, 1))),
            "query": bf(np.random.standard_normal((B, SQ, D))),
            "key": bf(np.random.standard_normal((B, SK, D)) * t[:, None]),
            "value": bf(np.random.standard_normal((B, SK, DV)) * 1.5 / np.sqrt(SK) / t[:, None])}


def reference(qk, qk_scaling_factor, query, key, value):
    gain = np.sqrt(D)
    scores = f64(query) @ f64(key).transpose(0, 2, 1)
    scores = scores / gain
    scores = scores / f64(qk_scaling_factor)
    scores = scores
    return mxq(scores, 2, "e4m3") @ mxq(f64(value), 1, "e4m3")

@@ -1,0 +1,234 @@
+import math
+from contextlib import ExitStack
+
+import concourse.mybir as mybir
+from concourse.masks import make_identity
+
+BF16 = mybir.dt.bfloat16
+F32 = mybir.dt.float32
+U32 = mybir.dt.uint32
+U8 = mybir.dt.uint8
+FP8X4 = mybir.dt.float8_e4m3fn_x4
+MULT = mybir.AluOpType.mult
+COPY = mybir.ActivationFunctionType.Copy
+
+P = 128
+SQ, SK, D, DV = 4096, 512, 128, 1024
+PACK = 4
+NB = SQ // P
+HALF = 512
+FLOPS = 2 * SQ * SK * D + 2 * SQ * SK * DV
+
+MANUAL = True
+LOOKAHEAD = 3
+HEAD = 3
+Q_CHUNKS = [(0, 4), (4, 8), (8, 16), (16, 32)]
+STORE_GROUPS = [1] * 9 + [2] * 9 + [1, 1]
+T_AT = {6: 2, 9: 3, 13: 4, 17: 5, 21: 6, 25: 7}
+VECTOR_SHARE = (1, 4, 6, 8, 11, 13, 15)
+
+
+def tile_model_t_kernel(tc, qk, qk_scaling_factor, query, key, value, out):
+    nc = tc.nc
+    with ExitStack() as ctx:
+        if MANUAL:
+            ctx.enter_context(tc.manual_schedule())
+        const = ctx.enter_context(tc.tile_pool(name="const", bufs=1))
+        work = ctx.enter_context(tc.tile_pool(name="work", bufs=8))
+        psum_t = ctx.enter_context(tc.psum_pool(name="psum_t", bufs=2))
+        psum_s = ctx.enter_context(tc.psum_pool(name="psum_s", bufs=2))
+        psum_o = ctx.enter_context(tc.psum_pool(name="psum_o", bufs=4))
+
+        q_view = query[0].rearrange("(p m) d -> p m d", m=NB)
+        k_view = key[0].rearrange("(p t) d -> p t d", t=PACK)
+        v_view = value[0].rearrange("(p t) n -> p t n", t=PACK)
+        o_view = out[0].rearrange("(p m) n -> p m n", m=NB)
+
+        sf_bf = const.tile([P, 1], BF16, name="sf_bf")
+        nc.scalar.dma_start(out=sf_bf[:], in_=qk_scaling_factor.rearrange("a b -> (a b)").partition_broadcast(P))
+        k_sb = const.tile([P, PACK, D], BF16, name="k_sb")
+        nc.sync.dma_start(out=k_sb[:], in_=k_view)
+        q_sb = {}
+
+        def load_q(c):
+            lo, hi = Q_CHUNKS[c]
+            t = const.tile([P, hi - lo, D], BF16, name="q_sb%d" % c)
+            nc.sync.dma_start(out=t[:], in_=q_view[:, lo:hi, :])
+            for m in range(lo, hi):
+                q_sb[m] = t[:, m - lo, :]
+
+        load_q(0)
+        v_src = {}
+
+        def load_v(lo, hi):
+            t = const.tile([P, PACK, hi - lo], BF16, name="v_sb%d" % lo)
+            nc.sync.dma_start(out=t[:], in_=v_view[:, :, lo:hi])
+            for c in range(lo, hi, 256):
+                v_src[c] = t[:, :, c - lo:c - lo + 256]
+
+        load_v(0, 256)
+        load_v(256, 512)
+        load_v(512, 1024)
+        for c in range(1, len(Q_CHUNKS)):
+            load_q(c)
+
+        ident = const.tile([P, P], BF16, name="ident")
+        make_identity(nc, ident[:])
+
+        sf_f = const.tile([P, 1], F32, name="sf_f")
+        nc.vector.tensor_scalar(out=sf_f[:], in0=sf_bf[:], scalar1=math.sqrt(float(D)), scalar2=None, op0=MULT)
+        inv = const.tile([P, 1], F32, name="inv")
+        nc.vector.reciprocal(out=inv[:], in_=sf_f[:])
+
+        k_ps = psum_t.tile([P, PACK, P], BF16, name="t_ps")
+        for t in range(PACK):
+            nc.tensor.transpose(k_ps[:, t, :], k_sb[:, t, :], ident[:])
+        kT = const.tile([P, PACK, P], BF16, name="kT")
+        nc.scalar.copy(out=kT[:], in_=k_ps[:])
+
+        qT = {}
+
+        def transposes(g, on_vector=False):
+            t_ps = psum_t.tile([P, 4, P], BF16, name="t_ps")
+            for j in range(4):
+                nc.tensor.transpose(t_ps[:, j, :], q_sb[4 * g + j], ident[:])
+            t = const.tile([P, 4, P], BF16, name="qT%d" % g)
+            if on_vector:
+                nc.vector.tensor_copy(out=t[:], in_=t_ps[:])
+            else:
+                nc.scalar.copy(out=t[:], in_=t_ps[:])
+            for j in range(4):
+                qT[4 * g + j] = t[:, j, :]
+
+        v_grp = const.tile([P, DV, PACK], BF16, name="v_grp", align_bytes=64)
+        v_codes = const.tile([P, DV], U32, name="v_codes", align_bytes=64)
+        v_scales = const.tile([P, DV], U8, name="v_scales", align_bytes=64)
+
+        def regroup_value(c):
+            nc.vector.tensor_copy(
+                out=v_grp[:, c:c + 256, :].rearrange("p (c i) t -> p c t i", i=4),
+                in_=v_src[c].rearrange("p t (c i) -> p c t i", i=4),
+            )
+
+        def quantise_value(lo, hi):
+            nc.vector.quantize_mx(
+                out=v_codes[:, lo:hi].bitcast(FP8X4),
+                scales=v_scales[:, lo:hi],
+                in_=v_grp[:, lo:hi, :].rearrange("p n t -> p (n t)"),
+            )
+
+        sc_ps, s_grp, s_codes, s_scales, acc_ps = {}, {}, {}, {}, {}
+
+        def scores(m):
+            sc = psum_s.tile([P, PACK, P], F32, name="sc")
+            for t in range(PACK):
+                nc.tensor.matmul(sc[:, t, :], lhsT=kT[:, t, :], rhs=qT[m], start=True, stop=True)
+            sc_ps[m] = sc
+
+        def scale_scores(m, on_vector=True):
+            grp = work.tile([P, P, PACK], BF16, name="grp", align_bytes=64)
+            src = sc_ps[m][:].rearrange("p t q -> p q t")
+            if on_vector:
+                nc.vector.tensor_scalar(out=grp[:], in0=src, scalar1=inv[:, 0:1], scalar2=None, op0=MULT)
+            else:
+                nc.scalar.activation(out=grp[:], in_=src, func=COPY, scale=inv[:, 0:1])
+            s_grp[m] = grp
+
+        def quantise_scores(m):
+            codes = work.tile([P, P], U32, name="codes", align_bytes=64)
+            scales = work.tile([P, P], U8, name="scales", align_bytes=64)
+            nc.vector.quantize_mx(
+                out=codes[:].bitcast(FP8X4), scales=scales[:], in_=s_grp[m][:].rearrange("p q t -> p (q t)")
+            )
+            s_codes[m] = codes
+            s_scales[m] = scales
+
+        def product(m, h):
+            acc = psum_o.tile([P, HALF], F32, name="acc")
+            nc.tensor.matmul_mx(
+                out=acc[:],
+                lhsT=s_codes[m][:].bitcast(FP8X4),
+                lhsT_scale=s_scales[m][:],
+                rhs=v_codes[:, h * HALF:(h + 1) * HALF].bitcast(FP8X4),
+                rhs_scale=v_scales[:, h * HALF:(h + 1) * HALF],
+                start=True,
+                stop=True,
+            )
+            acc_ps[(m, h)] = acc
+
+        group_of = {}
+        first = 0
+        for size in [1] * HEAD + STORE_GROUPS:
+            for m in range(first, first + size):
+                group_of[m] = (first, size)
+            first += size
+        assert first == NB
+        o_sb = {}
+
+        def copy_out(m, h, on_vector=False):
+            lo, size = group_of[m]
+            if lo not in o_sb:
+                o_sb[lo] = const.tile([P, size, DV], F32, name="o_sb%d" % lo)
+            dst = o_sb[lo][:, m - lo, h * HALF:(h + 1) * HALF]
+            if on_vector:
+                nc.vector.tensor_copy(out=dst, in_=acc_ps[(m, h)][:])
+            else:
+                nc.scalar.copy(out=dst, in_=acc_ps[(m, h)][:])
+
+        def store_half(m, h):
+            nc.sync.dma_start(out=o_view[:, m, h * HALF:(h + 1) * HALF], in_=o_sb[m][:, 0, h * HALF:(h + 1) * HALF])
+
+        def half(m, h):
+            product(m, h)
+            copy_out(m, h)
+            store_half(m, h)
+
+        transposes(0)
+        regroup_value(0)
+        quantise_value(0, 256)
+        scores(0)
+        scale_scores(0, on_vector=False)
+        scores(1)
+        scale_scores(1, on_vector=False)
+        regroup_value(256)
+        quantise_value(256, 512)
+        quantise_scores(0)
+        scores(2)
+        scale_scores(2, on_vector=False)
+        quantise_scores(1)
+        half(0, 0)
+        regroup_value(512)
+        quantise_scores(2)
+        scores(3)
+        half(1, 0)
+        regroup_value(768)
+        quantise_value(512, 1024)
+        transposes(1, on_vector=True)
+        half(2, 0)
+        scale_scores(3)
+        scores(4)
+        half(0, 1)
+        scale_scores(4)
+        quantise_scores(3)
+        scores(5)
+        half(1, 1)
+        scale_scores(5)
+        quantise_scores(4)
+        half(2, 1)
+
+        for m in range(HEAD, NB):
+            f = m + LOOKAHEAD
+            if f in T_AT:
+                transposes(T_AT[f])
+            if f < NB:
+                scores(f)
+                scale_scores(f)
+            if f - 1 < NB:
+                quantise_scores(f - 1)
+            product(m, 0)
+            product(m, 1)
+            copy_out(m, 0)
+            copy_out(m, 1, on_vector=(m % 16 in VECTOR_SHARE))
+            lo, size = group_of[m]
+            if m == lo + size - 1:
+                nc.sync.dma_start(out=o_view[:, lo:lo + size, :], in_=o_sb[lo][:])

@@ -21,10 +21,10 @@ FLOPS = 2 * SQ * SK * D + 2 * SQ * SK * DV
 
 MANUAL = True
 LOOKAHEAD = 3
-HEAD = 3
+HEAD = 4
 Q_CHUNKS = [(0, 4), (4, 8), (8, 16), (16, 32)]
-STORE_GROUPS = [1] * 9 + [2] * 9 + [1, 1]
-T_AT = {6: 2, 9: 3, 13: 4, 17: 5, 21: 6, 25: 7}
+STORE_GROUPS = [1] * 6 + [2] * 10 + [1, 1]
+T_AT = {9: 3, 13: 4, 17: 5, 21: 6, 25: 7}
 VECTOR_SHARE = (1, 4, 6, 8, 11, 13, 15)
 
 
@@ -84,7 +84,7 @@ def tile_model_t_kernel(tc, qk, qk_scaling_factor, query, key, value, out):
         for t in range(PACK):
             nc.tensor.transpose(k_ps[:, t, :], k_sb[:, t, :], ident[:])
         kT = const.tile([P, PACK, P], BF16, name="kT")
-        nc.scalar.copy(out=kT[:], in_=k_ps[:])
+        nc.vector.tensor_copy(out=kT[:], in_=k_ps[:])
 
         qT = {}
 
@@ -178,8 +178,7 @@ def tile_model_t_kernel(tc, qk, qk_scaling_factor, query, key, value, out):
         def store_half(m, h):
             nc.sync.dma_start(out=o_view[:, m, h * HALF:(h + 1) * HALF], in_=o_sb[m][:, 0, h * HALF:(h + 1) * HALF])
 
-        def half(m, h):
-            product(m, h)
+        def out_half(m, h):
             copy_out(m, h)
             store_half(m, h)
 
@@ -187,34 +186,48 @@ def tile_model_t_kernel(tc, qk, qk_scaling_factor, query, key, value, out):
         regroup_value(0)
         quantise_value(0, 256)
         scores(0)
-        scale_scores(0, on_vector=False)
         scores(1)
+        scale_scores(0, on_vector=False)
         scale_scores(1, on_vector=False)
         regroup_value(256)
         quantise_value(256, 512)
-        quantise_scores(0)
         scores(2)
+        scores(3)
         scale_scores(2, on_vector=False)
+        scale_scores(3, on_vector=False)
+        quantise_scores(0)
         quantise_scores(1)
-        half(0, 0)
+        product(0, 0)
+        product(1, 0)
         regroup_value(512)
         quantise_scores(2)
-        scores(3)
-        half(1, 0)
         regroup_value(768)
-        quantise_value(512, 1024)
-        transposes(1, on_vector=True)
-        half(2, 0)
-        scale_scores(3)
-        scores(4)
-        half(0, 1)
-        scale_scores(4)
         quantise_scores(3)
+        quantise_value(512, 1024)
+        out_half(0, 0)
+        out_half(1, 0)
+        transposes(1, on_vector=True)
+        product(2, 0)
+        product(3, 0)
+        out_half(2, 0)
+        out_half(3, 0)
+        product(0, 1)
+        scores(4)
+        product(1, 1)
         scores(5)
-        half(1, 1)
+        scale_scores(4)
+        out_half(0, 1)
         scale_scores(5)
         quantise_scores(4)
-        half(2, 1)
+        out_half(1, 1)
+        product(2, 1)
+        transposes(2)
+        scores(6)
+        product(3, 1)
+        scale_scores(6)
+        quantise_scores(5)
+        out_half(2, 1)
+        out_half(3, 1)
 
         for m in range(HEAD, NB):
             f = m + LOOKAHEAD

@@ -20,6 +20,7 @@ HALF = 512
 FLOPS = 2 * SQ * SK * D + 2 * SQ * SK * DV
 
 MANUAL = True
+WARM_UP = 5
 LOOKAHEAD = 3
 HEAD = 4
 Q_CHUNKS = [(0, 4), (4, 8), (8, 16), (16, 32)]
@@ -74,6 +75,16 @@ def tile_model_t_kernel(tc, qk, qk_scaling_factor, query, key, value, out):
 
         ident = const.tile([P, P], BF16, name="ident")
         make_identity(nc, ident[:])
+
+        warm = const.tile([P, HALF], BF16, name="warm")
+        nc.vector.memset(warm[:], 0.0)
+        warm_ps = psum_o.tile([P, HALF], F32, name="acc")
+
+        def dummies(n):
+            for i in range(n):
+                nc.tensor.matmul(warm_ps[:], lhsT=warm[:, 0:P], rhs=warm[:], start=True, stop=True)
+
+        dummies(WARM_UP)
 
         sf_f = const.tile([P, 1], F32, name="sf_f")
         nc.vector.tensor_scalar(out=sf_f[:], in0=sf_bf[:], scalar1=math.sqrt(float(D)), scalar2=None, op0=MULT)
@@ -183,10 +194,12 @@ def tile_model_t_kernel(tc, qk, qk_scaling_factor, query, key, value, out):
             store_half(m, h)
 
         transposes(0)
+        dummies(1)
         regroup_value(0)
         quantise_value(0, 256)
         scores(0)
         scores(1)
+        dummies(1)
         scale_scores(0, on_vector=False)
         scale_scores(1, on_vector=False)
         regroup_value(256)

@@ -26,7 +26,7 @@ HEAD = 4
 Q_CHUNKS = [(0, 4), (4, 8), (8, 16), (16, 32)]
 STORE_GROUPS = [1] * 6 + [2] * 10 + [1, 1]
 T_AT = {9: 3, 13: 4, 17: 5, 21: 6, 25: 7}
-VECTOR_SHARE = (1, 4, 6, 8, 11, 13, 15)
+VECTOR_SHARE = (1, 4, 7, 10, 13)
 
 
 def tile_model_t_kernel(tc, qk, qk_scaling_factor, query, key, value, out):

@@ -24,7 +24,7 @@ WARM_UP = 5
 LOOKAHEAD = 3
 HEAD = 4
 Q_CHUNKS = [(0, 4), (4, 8), (8, 16), (16, 32)]
-STORE_GROUPS = [1] * 6 + [2] * 10 + [1, 1]
+STORE_GROUPS = [1] * 4 + [2] * 8 + [4] * 2
 T_AT = {9: 3, 13: 4, 17: 5, 21: 6, 25: 7}
 VECTOR_SHARE = (1, 4, 7, 10, 13)
 

@@ -20,7 +20,7 @@ HALF = 512
 FLOPS = 2 * SQ * SK * D + 2 * SQ * SK * DV
 
 MANUAL = True
-WARM_UP = 5
+WARM_UP = 3
 LOOKAHEAD = 3
 HEAD = 4
 Q_CHUNKS = [(0, 4), (4, 8), (8, 16), (16, 32)]

@@ -45,8 +45,9 @@ def tile_model_t_kernel(tc, qk, qk_scaling_factor, query, key, value, out):
         v_view = value[0].rearrange("(p t) n -> p t n", t=PACK)
         o_view = out[0].rearrange("(p m) n -> p m n", m=NB)
 
-        sf_bf = const.tile([P, 1], BF16, name="sf_bf")
-        nc.scalar.dma_start(out=sf_bf[:], in_=qk_scaling_factor.rearrange("a b -> (a b)").partition_broadcast(P))
+        sf_row = const.tile([P, 2], BF16, name="sf_row")
+        nc.gpsimd.memset(sf_row[:], 0.0)
+        nc.scalar.dma_start(out=sf_row[0:1, 0:1], in_=qk_scaling_factor)
         k_sb = const.tile([P, PACK, D], BF16, name="k_sb")
         nc.sync.dma_start(out=k_sb[:], in_=k_view)
         q_sb = {}
@@ -79,6 +80,8 @@ def tile_model_t_kernel(tc, qk, qk_scaling_factor, query, key, value, out):
         warm = const.tile([P, HALF], BF16, name="warm")
         nc.vector.memset(warm[:], 0.0)
         warm_ps = psum_o.tile([P, HALF], F32, name="acc")
+        ones = const.tile([P, P], BF16, name="ones")
+        nc.vector.memset(ones[:], 1.0)
 
         def dummies(n):
             for i in range(n):
@@ -86,18 +89,26 @@ def tile_model_t_kernel(tc, qk, qk_scaling_factor, query, key, value, out):
 
         dummies(WARM_UP)
 
-        sf_f = const.tile([P, 1], F32, name="sf_f")
-        nc.vector.tensor_scalar(out=sf_f[:], in0=sf_bf[:], scalar1=math.sqrt(float(D)), scalar2=None, op0=MULT)
+        sf_ps = psum_o.tile([P, 2], F32, name="acc")
         inv = const.tile([P, 1], F32, name="inv")
-        nc.vector.reciprocal(out=inv[:], in_=sf_f[:])
 
-        k_ps = psum_t.tile([P, PACK, P], BF16, name="t_ps")
+        def spread_factor():
+            nc.tensor.matmul(sf_ps[:], lhsT=ones[:], rhs=sf_row[:], start=True, stop=True)
+
+        def invert_factor():
+            sf_f = const.tile([P, 1], F32, name="sf_f")
+            nc.vector.tensor_scalar(out=sf_f[:], in0=sf_ps[:, 0:1], scalar1=math.sqrt(float(D)), scalar2=None, op0=MULT)
+            nc.vector.reciprocal(out=inv[:], in_=sf_f[:])
+
+        kq_ps = psum_t.tile([P, PACK + 1, P], BF16, name="t_ps")
         for t in range(PACK):
-            nc.tensor.transpose(k_ps[:, t, :], k_sb[:, t, :], ident[:])
-        kT = const.tile([P, PACK, P], BF16, name="kT")
-        nc.vector.tensor_copy(out=kT[:], in_=k_ps[:])
+            nc.tensor.transpose(kq_ps[:, t, :], k_sb[:, t, :], ident[:])
+        nc.tensor.transpose(kq_ps[:, PACK, :], q_sb[0], ident[:])
+        kq = const.tile([P, PACK + 1, P], BF16, name="kq")
+        nc.scalar.copy(out=kq[:], in_=kq_ps[:])
+        kT = kq[:, 0:PACK, :]
 
-        qT = {}
+        qT = {0: kq[:, PACK, :]}
 
         def transposes(g, on_vector=False):
             t_ps = psum_t.tile([P, 4, P], BF16, name="t_ps")
@@ -110,6 +121,15 @@ def tile_model_t_kernel(tc, qk, qk_scaling_factor, query, key, value, out):
                 nc.scalar.copy(out=t[:], in_=t_ps[:])
             for j in range(4):
                 qT[4 * g + j] = t[:, j, :]
+
+        def first_transposes():
+            t_ps = psum_t.tile([P, 3, P], BF16, name="t_ps")
+            for j in range(1, 4):
+                nc.tensor.transpose(t_ps[:, j - 1, :], q_sb[j], ident[:])
+            t = const.tile([P, 3, P], BF16, name="qT0")
+            nc.scalar.copy(out=t[:], in_=t_ps[:])
+            for j in range(1, 4):
+                qT[j] = t[:, j - 1, :]
 
         v_grp = const.tile([P, DV, PACK], BF16, name="v_grp", align_bytes=64)
         v_codes = const.tile([P, DV], U32, name="v_codes", align_bytes=64)
@@ -193,22 +213,24 @@ def tile_model_t_kernel(tc, qk, qk_scaling_factor, query, key, value, out):
             copy_out(m, h)
             store_half(m, h)
 
-        transposes(0)
-        dummies(1)
+        first_transposes()
+        spread_factor()
         regroup_value(0)
+        invert_factor()
         quantise_value(0, 256)
         scores(0)
+        dummies(1)
         scores(1)
         dummies(1)
         scale_scores(0, on_vector=False)
         scale_scores(1, on_vector=False)
         regroup_value(256)
+        quantise_scores(0)
         quantise_value(256, 512)
         scores(2)
         scores(3)
         scale_scores(2, on_vector=False)
         scale_scores(3, on_vector=False)
-        quantise_scores(0)
         quantise_scores(1)
         product(0, 0)
         product(1, 0)

@@ -19,25 +19,22 @@ NB = SQ // P
 HALF = 512
 FLOPS = 2 * SQ * SK * D + 2 * SQ * SK * DV
 
-MANUAL = True
-WARM_UP = 3
+WARM_UP = 16
 LOOKAHEAD = 3
 HEAD = 4
 Q_CHUNKS = [(0, 4), (4, 8), (8, 16), (16, 32)]
 STORE_GROUPS = [1] * 4 + [2] * 8 + [4] * 2
-T_AT = {9: 3, 13: 4, 17: 5, 21: 6, 25: 7}
-VECTOR_SHARE = (1, 4, 7, 10, 13)
+TRANSPOSE_AT = {9: 3, 13: 4, 17: 5, 21: 6, 25: 7}
+VECTOR_SHARE = (1, 3, 6, 9, 11, 14)
 
 
 def tile_model_t_kernel(tc, qk, qk_scaling_factor, query, key, value, out):
     nc = tc.nc
     with ExitStack() as ctx:
-        if MANUAL:
-            ctx.enter_context(tc.manual_schedule())
+        ctx.enter_context(tc.manual_schedule())
         const = ctx.enter_context(tc.tile_pool(name="const", bufs=1))
         work = ctx.enter_context(tc.tile_pool(name="work", bufs=8))
-        psum_t = ctx.enter_context(tc.psum_pool(name="psum_t", bufs=2))
-        psum_s = ctx.enter_context(tc.psum_pool(name="psum_s", bufs=2))
+        psum_b = ctx.enter_context(tc.psum_pool(name="psum_b", bufs=4))
         psum_o = ctx.enter_context(tc.psum_pool(name="psum_o", bufs=4))
 
         q_view = query[0].rearrange("(p m) d -> p m d", m=NB)
@@ -77,17 +74,13 @@ def tile_model_t_kernel(tc, qk, qk_scaling_factor, query, key, value, out):
         ident = const.tile([P, P], BF16, name="ident")
         make_identity(nc, ident[:])
 
-        warm = const.tile([P, HALF], BF16, name="warm")
-        nc.vector.memset(warm[:], 0.0)
-        warm_ps = psum_o.tile([P, HALF], F32, name="acc")
         ones = const.tile([P, P], BF16, name="ones")
         nc.vector.memset(ones[:], 1.0)
+        warm_ps = psum_o.tile([P, P], F32, name="acc")
 
         def dummies(n):
             for i in range(n):
-                nc.tensor.matmul(warm_ps[:], lhsT=warm[:, 0:P], rhs=warm[:], start=True, stop=True)
-
-        dummies(WARM_UP)
+                nc.tensor.matmul(warm_ps[:], lhsT=ones[:], rhs=ones[:], start=True, stop=True)
 
         sf_ps = psum_o.tile([P, 2], F32, name="acc")
         inv = const.tile([P, 1], F32, name="inv")
@@ -100,36 +93,29 @@ def tile_model_t_kernel(tc, qk, qk_scaling_factor, query, key, value, out):
             nc.vector.tensor_scalar(out=sf_f[:], in0=sf_ps[:, 0:1], scalar1=math.sqrt(float(D)), scalar2=None, op0=MULT)
             nc.vector.reciprocal(out=inv[:], in_=sf_f[:])
 
-        kq_ps = psum_t.tile([P, PACK + 1, P], BF16, name="t_ps")
-        for t in range(PACK):
-            nc.tensor.transpose(kq_ps[:, t, :], k_sb[:, t, :], ident[:])
-        nc.tensor.transpose(kq_ps[:, PACK, :], q_sb[0], ident[:])
-        kq = const.tile([P, PACK + 1, P], BF16, name="kq")
-        nc.scalar.copy(out=kq[:], in_=kq_ps[:])
-        kT = kq[:, 0:PACK, :]
+        qT = {}
+        qT_ps = {}
 
-        qT = {0: kq[:, PACK, :]}
+        def transpose_key():
+            t_ps = psum_b.tile([P, PACK, P], BF16, name="bank")
+            for t in range(PACK):
+                nc.tensor.transpose(t_ps[:, t, :], k_sb[:, t, :], ident[:])
+            return t_ps
 
-        def transposes(g, on_vector=False):
-            t_ps = psum_t.tile([P, 4, P], BF16, name="t_ps")
-            for j in range(4):
-                nc.tensor.transpose(t_ps[:, j, :], q_sb[4 * g + j], ident[:])
-            t = const.tile([P, 4, P], BF16, name="qT%d" % g)
+        def transpose_query(lo, hi):
+            t_ps = psum_b.tile([P, hi - lo, P], BF16, name="bank")
+            for m in range(lo, hi):
+                nc.tensor.transpose(t_ps[:, m - lo, :], q_sb[m], ident[:])
+            qT_ps[lo] = t_ps
+
+        def copy_query(lo, hi, on_vector=False):
+            t = const.tile([P, hi - lo, P], BF16, name="qT%d" % lo)
             if on_vector:
-                nc.vector.tensor_copy(out=t[:], in_=t_ps[:])
+                nc.vector.tensor_copy(out=t[:], in_=qT_ps[lo][:])
             else:
-                nc.scalar.copy(out=t[:], in_=t_ps[:])
-            for j in range(4):
-                qT[4 * g + j] = t[:, j, :]
-
-        def first_transposes():
-            t_ps = psum_t.tile([P, 3, P], BF16, name="t_ps")
-            for j in range(1, 4):
-                nc.tensor.transpose(t_ps[:, j - 1, :], q_sb[j], ident[:])
-            t = const.tile([P, 3, P], BF16, name="qT0")
-            nc.scalar.copy(out=t[:], in_=t_ps[:])
-            for j in range(1, 4):
-                qT[j] = t[:, j - 1, :]
+                nc.scalar.copy(out=t[:], in_=qT_ps[lo][:])
+            for m in range(lo, hi):
+                qT[m] = t[:, m - lo, :]
 
         v_grp = const.tile([P, DV, PACK], BF16, name="v_grp", align_bytes=64)
         v_codes = const.tile([P, DV], U32, name="v_codes", align_bytes=64)
@@ -151,7 +137,7 @@ def tile_model_t_kernel(tc, qk, qk_scaling_factor, query, key, value, out):
         sc_ps, s_grp, s_codes, s_scales, acc_ps = {}, {}, {}, {}, {}
 
         def scores(m):
-            sc = psum_s.tile([P, PACK, P], F32, name="sc")
+            sc = psum_b.tile([P, PACK, P], F32, name="bank")
             for t in range(PACK):
                 nc.tensor.matmul(sc[:, t, :], lhsT=kT[:, t, :], rhs=qT[m], start=True, stop=True)
             sc_ps[m] = sc
@@ -174,18 +160,18 @@ def tile_model_t_kernel(tc, qk, qk_scaling_factor, query, key, value, out):
             s_codes[m] = codes
             s_scales[m] = scales
 
-        def product(m, h):
-            acc = psum_o.tile([P, HALF], F32, name="acc")
+        def product(m, lo, hi):
+            acc = psum_o.tile([P, hi - lo], F32, name="acc")
             nc.tensor.matmul_mx(
                 out=acc[:],
                 lhsT=s_codes[m][:].bitcast(FP8X4),
                 lhsT_scale=s_scales[m][:],
-                rhs=v_codes[:, h * HALF:(h + 1) * HALF].bitcast(FP8X4),
-                rhs_scale=v_scales[:, h * HALF:(h + 1) * HALF],
+                rhs=v_codes[:, lo:hi].bitcast(FP8X4),
+                rhs_scale=v_scales[:, lo:hi],
                 start=True,
                 stop=True,
             )
-            acc_ps[(m, h)] = acc
+            acc_ps[(m, lo)] = acc
 
         group_of = {}
         first = 0
@@ -196,87 +182,97 @@ def tile_model_t_kernel(tc, qk, qk_scaling_factor, query, key, value, out):
         assert first == NB
         o_sb = {}
 
-        def copy_out(m, h, on_vector=False):
+        def copy_out(m, c, hi, on_vector=False):
             lo, size = group_of[m]
             if lo not in o_sb:
                 o_sb[lo] = const.tile([P, size, DV], F32, name="o_sb%d" % lo)
-            dst = o_sb[lo][:, m - lo, h * HALF:(h + 1) * HALF]
+            dst = o_sb[lo][:, m - lo, c:hi]
             if on_vector:
-                nc.vector.tensor_copy(out=dst, in_=acc_ps[(m, h)][:])
+                nc.vector.tensor_copy(out=dst, in_=acc_ps[(m, c)][:])
             else:
-                nc.scalar.copy(out=dst, in_=acc_ps[(m, h)][:])
+                nc.scalar.copy(out=dst, in_=acc_ps[(m, c)][:])
 
-        def store_half(m, h):
-            nc.sync.dma_start(out=o_view[:, m, h * HALF:(h + 1) * HALF], in_=o_sb[m][:, 0, h * HALF:(h + 1) * HALF])
+        def out_part(m, c, hi, on_vector=False):
+            copy_out(m, c, hi, on_vector)
+            nc.sync.dma_start(out=o_view[:, m, c:hi], in_=o_sb[m][:, 0, c:hi])
 
-        def out_half(m, h):
-            copy_out(m, h)
-            store_half(m, h)
-
-        first_transposes()
+        dummies(WARM_UP)
+        k_ps = transpose_key()
+        transpose_query(0, 1)
+        kT_sb = const.tile([P, PACK, P], BF16, name="kT_sb")
+        nc.scalar.copy(out=kT_sb[:], in_=k_ps[:])
+        kT = kT_sb
+        copy_query(0, 1, on_vector=True)
         spread_factor()
-        regroup_value(0)
+        transpose_query(1, 4)
         invert_factor()
-        quantise_value(0, 256)
+        copy_query(1, 4)
+        dummies(2)
         scores(0)
-        dummies(1)
+        regroup_value(0)
         scores(1)
-        dummies(1)
         scale_scores(0, on_vector=False)
-        scale_scores(1, on_vector=False)
-        regroup_value(256)
-        quantise_scores(0)
-        quantise_value(256, 512)
+        quantise_value(0, 256)
         scores(2)
+        scale_scores(1, on_vector=False)
         scores(3)
+        regroup_value(256)
         scale_scores(2, on_vector=False)
-        scale_scores(3, on_vector=False)
+        quantise_scores(0)
+        product(0, 0, 256)
+        out_part(0, 0, 256)
+        quantise_value(256, 512)
+        product(0, 256, 512)
+        out_part(0, 256, 512)
         quantise_scores(1)
-        product(0, 0)
-        product(1, 0)
+        product(1, 0, 512)
+        out_part(1, 0, 512)
         regroup_value(512)
+        transpose_query(4, 8)
         quantise_scores(2)
+        product(2, 0, 512)
+        scale_scores(3, on_vector=False)
         regroup_value(768)
-        quantise_scores(3)
+        out_part(2, 0, 512)
+        copy_query(4, 8, on_vector=True)
         quantise_value(512, 1024)
-        out_half(0, 0)
-        out_half(1, 0)
-        transposes(1, on_vector=True)
-        product(2, 0)
-        product(3, 0)
-        out_half(2, 0)
-        out_half(3, 0)
-        product(0, 1)
+        quantise_scores(3)
         scores(4)
-        product(1, 1)
+        product(0, 512, 1024)
+        product(3, 0, 512)
         scores(5)
+        out_part(0, 512, 1024)
         scale_scores(4)
-        out_half(0, 1)
-        scale_scores(5)
+        product(1, 512, 1024)
+        out_part(3, 0, 512, on_vector=True)
+        out_part(1, 512, 1024)
+        product(2, 512, 1024)
         quantise_scores(4)
-        out_half(1, 1)
-        product(2, 1)
-        transposes(2)
-        scores(6)
-        product(3, 1)
-        scale_scores(6)
+        out_part(2, 512, 1024)
+        scale_scores(5)
+        product(3, 512, 1024)
+        transpose_query(8, 12)
         quantise_scores(5)
-        out_half(2, 1)
-        out_half(3, 1)
+        out_part(3, 512, 1024)
+        copy_query(8, 12)
+        scores(6)
+        scale_scores(6)
 
         for m in range(HEAD, NB):
             f = m + LOOKAHEAD
-            if f in T_AT:
-                transposes(T_AT[f])
+            if f in TRANSPOSE_AT:
+                g = TRANSPOSE_AT[f]
+                transpose_query(4 * g, 4 * g + 4)
+                copy_query(4 * g, 4 * g + 4)
             if f < NB:
                 scores(f)
                 scale_scores(f)
             if f - 1 < NB:
                 quantise_scores(f - 1)
-            product(m, 0)
-            product(m, 1)
-            copy_out(m, 0)
-            copy_out(m, 1, on_vector=(m % 16 in VECTOR_SHARE))
+            product(m, 0, HALF)
+            product(m, HALF, DV)
+            copy_out(m, 0, HALF)
+            copy_out(m, HALF, DV, on_vector=(m % 16 in VECTOR_SHARE))
             lo, size = group_of[m]
             if m == lo + size - 1:
                 nc.sync.dma_start(out=o_view[:, lo:lo + size, :], in_=o_sb[lo][:])

@@ -67,9 +67,11 @@ def tile_model_t_kernel(tc, qk, qk_scaling_factor, query, key, value, out):
 
         load_v(0, 256)
         load_v(256, 512)
-        load_v(512, 1024)
-        for c in range(1, len(Q_CHUNKS)):
-            load_q(c)
+        load_q(1)
+        load_v(512, 768)
+        load_v(768, 1024)
+        load_q(2)
+        load_q(3)
 
         ident = const.tile([P, P], BF16, name="ident")
         make_identity(nc, ident[:])
@@ -218,6 +220,8 @@ def tile_model_t_kernel(tc, qk, qk_scaling_factor, query, key, value, out):
         scores(3)
         regroup_value(256)
         scale_scores(2, on_vector=False)
+        scale_scores(3, on_vector=False)
+        transpose_query(4, 8)
         quantise_scores(0)
         product(0, 0, 256)
         out_part(0, 0, 256)
@@ -227,36 +231,34 @@ def tile_model_t_kernel(tc, qk, qk_scaling_factor, query, key, value, out):
         quantise_scores(1)
         product(1, 0, 512)
         out_part(1, 0, 512)
+        copy_query(4, 8, on_vector=True)
         regroup_value(512)
-        transpose_query(4, 8)
+        scores(4)
         quantise_scores(2)
         product(2, 0, 512)
-        scale_scores(3, on_vector=False)
-        regroup_value(768)
         out_part(2, 0, 512)
-        copy_query(4, 8, on_vector=True)
-        quantise_value(512, 1024)
         quantise_scores(3)
-        scores(4)
-        product(0, 512, 1024)
-        product(3, 0, 512)
+        regroup_value(768)
         scores(5)
-        out_part(0, 512, 1024)
+        product(3, 0, 512)
+        out_part(3, 0, 512)
+        quantise_value(512, 1024)
         scale_scores(4)
+        product(0, 512, 1024)
+        scale_scores(5, on_vector=False)
         product(1, 512, 1024)
-        out_part(3, 0, 512, on_vector=True)
-        out_part(1, 512, 1024)
-        product(2, 512, 1024)
+        out_part(0, 512, 1024)
         quantise_scores(4)
+        product(2, 512, 1024)
+        out_part(1, 512, 1024, on_vector=True)
         out_part(2, 512, 1024)
-        scale_scores(5)
         product(3, 512, 1024)
-        transpose_query(8, 12)
         quantise_scores(5)
-        out_part(3, 512, 1024)
-        copy_query(8, 12)
         scores(6)
+        out_part(3, 512, 1024, on_vector=True)
         scale_scores(6)
+        transpose_query(8, 12)
+        copy_query(8, 12)
 
         for m in range(HEAD, NB):
             f = m + LOOKAHEAD

@@ -232,16 +232,17 @@ def tile_model_t_kernel(tc, qk, qk_scaling_factor, query, key, value, out):
         product(1, 0, 512)
         out_part(1, 0, 512)
         copy_query(4, 8, on_vector=True)
-        regroup_value(512)
-        scores(4)
         quantise_scores(2)
         product(2, 0, 512)
         out_part(2, 0, 512)
+        scores(4)
+        regroup_value(512)
         quantise_scores(3)
-        regroup_value(768)
-        scores(5)
         product(3, 0, 512)
         out_part(3, 0, 512)
+        scores(5)
+        regroup_value(768)
+        scores(6)
         quantise_value(512, 1024)
         scale_scores(4)
         product(0, 512, 1024)
@@ -249,15 +250,14 @@ def tile_model_t_kernel(tc, qk, qk_scaling_factor, query, key, value, out):
         product(1, 512, 1024)
         out_part(0, 512, 1024)
         quantise_scores(4)
+        scale_scores(6)
         product(2, 512, 1024)
         out_part(1, 512, 1024, on_vector=True)
         out_part(2, 512, 1024)
         product(3, 512, 1024)
         quantise_scores(5)
-        scores(6)
-        out_part(3, 512, 1024, on_vector=True)
-        scale_scores(6)
         transpose_query(8, 12)
+        out_part(3, 512, 1024, on_vector=True)
         copy_query(8, 12)
 
         for m in range(HEAD, NB):

@@ -22,7 +22,7 @@ FLOPS = 2 * SQ * SK * D + 2 * SQ * SK * DV
 WARM_UP = 16
 LOOKAHEAD = 3
 HEAD = 4
-Q_CHUNKS = [(0, 4), (4, 8), (8, 16), (16, 32)]
+Q_CHUNKS = [(0, 4), (4, 8), (8, 32)]
 STORE_GROUPS = [1] * 4 + [2] * 8 + [4] * 2
 TRANSPOSE_AT = {9: 3, 13: 4, 17: 5, 21: 6, 25: 7}
 VECTOR_SHARE = (1, 3, 6, 9, 11, 14)
@@ -65,13 +65,10 @@ def tile_model_t_kernel(tc, qk, qk_scaling_factor, query, key, value, out):
             for c in range(lo, hi, 256):
                 v_src[c] = t[:, :, c - lo:c - lo + 256]
 
-        load_v(0, 256)
-        load_v(256, 512)
+        load_v(0, 512)
         load_q(1)
-        load_v(512, 768)
-        load_v(768, 1024)
+        load_v(512, 1024)
         load_q(2)
-        load_q(3)
 
         ident = const.tile([P, P], BF16, name="ident")
         make_identity(nc, ident[:])
@@ -214,11 +211,11 @@ def tile_model_t_kernel(tc, qk, qk_scaling_factor, query, key, value, out):
         regroup_value(0)
         scores(1)
         scale_scores(0, on_vector=False)
-        quantise_value(0, 256)
         scores(2)
         scale_scores(1, on_vector=False)
         scores(3)
         regroup_value(256)
+        quantise_value(0, 256)
         scale_scores(2, on_vector=False)
         scale_scores(3, on_vector=False)
         transpose_query(4, 8)

@@ -19,7 +19,7 @@ NB = SQ // P
 HALF = 512
 FLOPS = 2 * SQ * SK * D + 2 * SQ * SK * DV
 
-WARM_UP = 16
+WARM_UP = 4
 LOOKAHEAD = 3
 HEAD = 4
 Q_CHUNKS = [(0, 4), (4, 8), (8, 32)]
@@ -75,11 +75,11 @@ def tile_model_t_kernel(tc, qk, qk_scaling_factor, query, key, value, out):
 
         ones = const.tile([P, P], BF16, name="ones")
         nc.vector.memset(ones[:], 1.0)
-        warm_ps = psum_o.tile([P, P], F32, name="acc")
+        warm_ps = psum_o.tile([P, HALF], F32, name="acc")
 
         def dummies(n):
             for i in range(n):
-                nc.tensor.matmul(warm_ps[:], lhsT=ones[:], rhs=ones[:], start=True, stop=True)
+                nc.tensor.matmul(warm_ps[:], lhsT=ones[:], rhs=ones[:, 0:1].to_broadcast([P, HALF]), start=True, stop=True)
 
         sf_ps = psum_o.tile([P, 2], F32, name="acc")
         inv = const.tile([P, 1], F32, name="inv")
@@ -206,7 +206,6 @@ def tile_model_t_kernel(tc, qk, qk_scaling_factor, query, key, value, out):
         transpose_query(1, 4)
         invert_factor()
         copy_query(1, 4)
-        dummies(2)
         scores(0)
         regroup_value(0)
         scores(1)

import math
from contextlib import ExitStack

import concourse.mybir as mybir
from concourse.masks import make_identity

BF16 = mybir.dt.bfloat16
F32 = mybir.dt.float32
U32 = mybir.dt.uint32
U8 = mybir.dt.uint8
FP8X4 = mybir.dt.float8_e4m3fn_x4
MULT = mybir.AluOpType.mult
COPY = mybir.ActivationFunctionType.Copy

P = 128
SQ, SK, D, DV = 4096, 512, 128, 1024
PACK = 4
NB = SQ // P
HALF = 512
FLOPS = 2 * SQ * SK * D + 2 * SQ * SK * DV

WARM_UP = 4
LOOKAHEAD = 3
HEAD = 4
Q_CHUNKS = [(0, 4), (4, 8), (8, 32)]
STORE_GROUPS = [1] * 4 + [2] * 8 + [4] * 2
TRANSPOSE_AT = {9: 3, 13: 4, 17: 5, 21: 6, 25: 7}
VECTOR_SHARE = (1, 3, 6, 9, 11, 14)


def tile_model_t_kernel(tc, qk, qk_scaling_factor, query, key, value, out):
    nc = tc.nc
    with ExitStack() as ctx:
        ctx.enter_context(tc.manual_schedule())
        const = ctx.enter_context(tc.tile_pool(name="const", bufs=1))
        work = ctx.enter_context(tc.tile_pool(name="work", bufs=8))
        psum_b = ctx.enter_context(tc.psum_pool(name="psum_b", bufs=4))
        psum_o = ctx.enter_context(tc.psum_pool(name="psum_o", bufs=4))

        q_view = query[0].rearrange("(p m) d -> p m d", m=NB)
        k_view = key[0].rearrange("(p t) d -> p t d", t=PACK)
        v_view = value[0].rearrange("(p t) n -> p t n", t=PACK)
        o_view = out[0].rearrange("(p m) n -> p m n", m=NB)

        sf_row = const.tile([P, 2], BF16, name="sf_row")
        nc.gpsimd.memset(sf_row[:], 0.0)
        nc.scalar.dma_start(out=sf_row[0:1, 0:1], in_=qk_scaling_factor)
        k_sb = const.tile([P, PACK, D], BF16, name="k_sb")
        nc.sync.dma_start(out=k_sb[:], in_=k_view)
        q_sb = {}

        def load_q(c):
            lo, hi = Q_CHUNKS[c]
            t = const.tile([P, hi - lo, D], BF16, name="q_sb%d" % c)
            nc.sync.dma_start(out=t[:], in_=q_view[:, lo:hi, :])
            for m in range(lo, hi):
                q_sb[m] = t[:, m - lo, :]

        load_q(0)
        v_src = {}

        def load_v(lo, hi):
            t = const.tile([P, PACK, hi - lo], BF16, name="v_sb%d" % lo)
            nc.sync.dma_start(out=t[:], in_=v_view[:, :, lo:hi])
            for c in range(lo, hi, 256):
                v_src[c] = t[:, :, c - lo:c - lo + 256]

        load_v(0, 512)
        load_q(1)
        load_v(512, 1024)
        load_q(2)

        ident = const.tile([P, P], BF16, name="ident")
        make_identity(nc, ident[:])

        ones = const.tile([P, P], BF16, name="ones")
        nc.vector.memset(ones[:], 1.0)
        warm_ps = psum_o.tile([P, HALF], F32, name="acc")

        def dummies(n):
            for i in range(n):
                nc.tensor.matmul(warm_ps[:], lhsT=ones[:], rhs=ones[:, 0:1].to_broadcast([P, HALF]), start=True, stop=True)

        sf_ps = psum_o.tile([P, 2], F32, name="acc")
        inv = const.tile([P, 1], F32, name="inv")

        def spread_factor():
            nc.tensor.matmul(sf_ps[:], lhsT=ones[:], rhs=sf_row[:], start=True, stop=True)

        def invert_factor():
            sf_f = const.tile([P, 1], F32, name="sf_f")
            nc.vector.tensor_scalar(out=sf_f[:], in0=sf_ps[:, 0:1], scalar1=math.sqrt(float(D)), scalar2=None, op0=MULT)
            nc.vector.reciprocal(out=inv[:], in_=sf_f[:])

        qT = {}
        qT_ps = {}

        def transpose_key():
            t_ps = psum_b.tile([P, PACK, P], BF16, name="bank")
            for t in range(PACK):
                nc.tensor.transpose(t_ps[:, t, :], k_sb[:, t, :], ident[:])
            return t_ps

        def transpose_query(lo, hi):
            t_ps = psum_b.tile([P, hi - lo, P], BF16, name="bank")
            for m in range(lo, hi):
                nc.tensor.transpose(t_ps[:, m - lo, :], q_sb[m], ident[:])
            qT_ps[lo] = t_ps

        def copy_query(lo, hi, on_vector=False):
            t = const.tile([P, hi - lo, P], BF16, name="qT%d" % lo)
            if on_vector:
                nc.vector.tensor_copy(out=t[:], in_=qT_ps[lo][:])
            else:
                nc.scalar.copy(out=t[:], in_=qT_ps[lo][:])
            for m in range(lo, hi):
                qT[m] = t[:, m - lo, :]

        v_grp = const.tile([P, DV, PACK], BF16, name="v_grp", align_bytes=64)
        v_codes = const.tile([P, DV], U32, name="v_codes", align_bytes=64)
        v_scales = const.tile([P, DV], U8, name="v_scales", align_bytes=64)

        def regroup_value(c):
            nc.vector.tensor_copy(
                out=v_grp[:, c:c + 256, :].rearrange("p (c i) t -> p c t i", i=4),
                in_=v_src[c].rearrange("p t (c i) -> p c t i", i=4),
            )

        def quantise_value(lo, hi):
            nc.vector.quantize_mx(
                out=v_codes[:, lo:hi].bitcast(FP8X4),
                scales=v_scales[:, lo:hi],
                in_=v_grp[:, lo:hi, :].rearrange("p n t -> p (n t)"),
            )

        sc_ps, s_grp, s_codes, s_scales, acc_ps = {}, {}, {}, {}, {}

        def scores(m):
            sc = psum_b.tile([P, PACK, P], F32, name="bank")
            for t in range(PACK):
                nc.tensor.matmul(sc[:, t, :], lhsT=kT[:, t, :], rhs=qT[m], start=True, stop=True)
            sc_ps[m] = sc

        def scale_scores(m, on_vector=True):
            grp = work.tile([P, P, PACK], BF16, name="grp", align_bytes=64)
            src = sc_ps[m][:].rearrange("p t q -> p q t")
            if on_vector:
                nc.vector.tensor_scalar(out=grp[:], in0=src, scalar1=inv[:, 0:1], scalar2=None, op0=MULT)
            else:
                nc.scalar.activation(out=grp[:], in_=src, func=COPY, scale=inv[:, 0:1])
            s_grp[m] = grp

        def quantise_scores(m):
            codes = work.tile([P, P], U32, name="codes", align_bytes=64)
            scales = work.tile([P, P], U8, name="scales", align_bytes=64)
            nc.vector.quantize_mx(
                out=codes[:].bitcast(FP8X4), scales=scales[:], in_=s_grp[m][:].rearrange("p q t -> p (q t)")
            )
            s_codes[m] = codes
            s_scales[m] = scales

        def product(m, lo, hi):
            acc = psum_o.tile([P, hi - lo], F32, name="acc")
            nc.tensor.matmul_mx(
                out=acc[:],
                lhsT=s_codes[m][:].bitcast(FP8X4),
                lhsT_scale=s_scales[m][:],
                rhs=v_codes[:, lo:hi].bitcast(FP8X4),
                rhs_scale=v_scales[:, lo:hi],
                start=True,
                stop=True,
            )
            acc_ps[(m, lo)] = acc

        group_of = {}
        first = 0
        for size in [1] * HEAD + STORE_GROUPS:
            for m in range(first, first + size):
                group_of[m] = (first, size)
            first += size
        assert first == NB
        o_sb = {}

        def copy_out(m, c, hi, on_vector=False):
            lo, size = group_of[m]
            if lo not in o_sb:
                o_sb[lo] = const.tile([P, size, DV], F32, name="o_sb%d" % lo)
            dst = o_sb[lo][:, m - lo, c:hi]
            if on_vector:
                nc.vector.tensor_copy(out=dst, in_=acc_ps[(m, c)][:])
            else:
                nc.scalar.copy(out=dst, in_=acc_ps[(m, c)][:])

        def out_part(m, c, hi, on_vector=False):
            copy_out(m, c, hi, on_vector)
            nc.sync.dma_start(out=o_view[:, m, c:hi], in_=o_sb[m][:, 0, c:hi])

        dummies(WARM_UP)
        k_ps = transpose_key()
        transpose_query(0, 1)
        kT_sb = const.tile([P, PACK, P], BF16, name="kT_sb")
        nc.scalar.copy(out=kT_sb[:], in_=k_ps[:])
        kT = kT_sb
        copy_query(0, 1, on_vector=True)
        spread_factor()
        transpose_query(1, 4)
        invert_factor()
        copy_query(1, 4)
        scores(0)
        regroup_value(0)
        scores(1)
        scale_scores(0, on_vector=False)
        scores(2)
        scale_scores(1, on_vector=False)
        scores(3)
        regroup_value(256)
        quantise_value(0, 256)
        scale_scores(2, on_vector=False)
        scale_scores(3, on_vector=False)
        transpose_query(4, 8)
        quantise_scores(0)
        product(0, 0, 256)
        out_part(0, 0, 256)
        quantise_value(256, 512)
        product(0, 256, 512)
        out_part(0, 256, 512)
        quantise_scores(1)
        product(1, 0, 512)
        out_part(1, 0, 512)
        copy_query(4, 8, on_vector=True)
        quantise_scores(2)
        product(2, 0, 512)
        out_part(2, 0, 512)
        scores(4)
        regroup_value(512)
        quantise_scores(3)
        product(3, 0, 512)
        out_part(3, 0, 512)
        scores(5)
        regroup_value(768)
        scores(6)
        quantise_value(512, 1024)
        scale_scores(4)
        product(0, 512, 1024)
        scale_scores(5, on_vector=False)
        product(1, 512, 1024)
        out_part(0, 512, 1024)
        quantise_scores(4)
        scale_scores(6)
        product(2, 512, 1024)
        out_part(1, 512, 1024, on_vector=True)
        out_part(2, 512, 1024)
        product(3, 512, 1024)
        quantise_scores(5)
        transpose_query(8, 12)
        out_part(3, 512, 1024, on_vector=True)
        copy_query(8, 12)

        for m in range(HEAD, NB):
            f = m + LOOKAHEAD
            if f in TRANSPOSE_AT:
                g = TRANSPOSE_AT[f]
                transpose_query(4 * g, 4 * g + 4)
                copy_query(4 * g, 4 * g + 4)
            if f < NB:
                scores(f)
                scale_scores(f)
            if f - 1 < NB:
                quantise_scores(f - 1)
            product(m, 0, HALF)
            product(m, HALF, DV)
            copy_out(m, 0, HALF)
            copy_out(m, HALF, DV, on_vector=(m % 16 in VECTOR_SHARE))
            lo, size = group_of[m]
            if m == lo + size - 1:
                nc.sync.dma_start(out=o_view[:, lo:lo + size, :], in_=o_sb[lo][:])
